import numpy as np
import ml_dtypes

BF16 = ml_dtypes.bfloat16


def bf(x):
    return np.asarray(x, np.float32).astype(BF16)


def f32(x):
    return np.asarray(x, np.float32)


def f64(x):
    return np.asarray(x).astype(np.float64)


def striped(idx):
    return np.tile(idx.reshape(-1, 16).T, (8, 1))


C, S, N, Q, L, K, HOPS = 1024, 4096, 2048, 256, 8, 128, 6
B_ATT = 0.5


def setup_inputs():
    loc = np.random.permutation(np.tile(np.arange(L), Q // L))
    v = 1.0 - np.abs(np.arange(L)[None, :] - loc[:, None]) / L
    return {
        "emb": f32(np.random.standard_normal((C, S))),
        "v_loc": f32(v).reshape(1, N),
        "aspect": f32(np.random.standard_normal((C, Q))),
        "w_mem": bf(1.5 * np.random.standard_normal((C, 1)) / np.sqrt(C)),
        "w_vec": bf(1.5 * np.random.standard_normal((C, 1)) / np.sqrt(C)),
        "w_lin": bf(0.7 * np.random.standard_normal((C, C)) / np.sqrt(C)),
        "b_lin": f32(0.2 * np.random.standard_normal((C, 1))),
        "w_out": bf(2.0 * np.random.standard_normal((C, K)) / np.sqrt(C)),
        "b_out": f32(0.2 * np.random.standard_normal((K, 1))),
        "offs": striped(np.random.permutation(np.tile(np.arange(S), 2))[:N]),
    }


def reference(emb, v_loc, aspect, w_mem, w_vec, w_lin, b_lin, w_out, b_out, offs):
    idx = offs[:16].T.reshape(-1)
    ext = f64(emb)[:, idx] * f64(v_loc)
    e = (f64(w_mem) * ext).sum(axis=0).reshape(Q, L)
    ext3 = ext.reshape(C, Q, L)
    vec = f64(aspect)
    for _ in range(HOPS):
        u = (f64(w_vec) * vec).sum(axis=0)
        p = np.exp(np.tanh(e + u[:, None] + B_ATT))
        alpha = p / p.sum(axis=1, keepdims=True)
        att = (ext3 * alpha[None, :, :]).sum(axis=2)
        vec = att + f64(w_lin).T @ vec + f64(b_lin)
    return f64(w_out).T @ vec + f64(b_out)

@@ -1,0 +1,177 @@
+import concourse.mybir as mybir
+from concourse.masks import make_identity
+
+F32, BF16, U16 = mybir.dt.float32, mybir.dt.bfloat16, mybir.dt.uint16
+MULT, ADD = mybir.AluOpType.mult, mybir.AluOpType.add
+ACT = mybir.ActivationFunctionType
+
+P = 128
+C, S, N, Q, L, K, HOPS = 1024, 4096, 2048, 256, 8, 128, 6
+B_ATT = 0.5
+CB = C // P
+QB = Q // P
+NB = N // QB
+BANK = 512
+FLIPS = BANK // P
+HALVES = C // BANK
+
+FLOPS = 2 * C * N + HOPS * (2 * C * Q + 2 * C * C * Q + 2 * C * N) + 2 * C * K * Q
+
+
+def tile_memnet_b_kernel(
+    tc, emb, v_loc, aspect, w_mem, w_vec, w_lin, b_lin, w_out, b_out, offs, out
+):
+    nc = tc.nc
+    with (
+        tc.tile_pool(name="held", bufs=1) as held,
+        tc.tile_pool(name="windows", bufs=3) as windows,
+        tc.tile_pool(name="picked", bufs=4) as picked,
+        tc.tile_pool(name="vecs", bufs=2 * QB) as vecs,
+        tc.tile_pool(name="small", bufs=2 * QB) as small,
+        tc.tile_pool(name="sums", bufs=3) as sums,
+        tc.tile_pool(name="rows", bufs=2) as rows,
+        tc.psum_pool(name="psum", bufs=2) as psum,
+    ):
+        offsets = held.tile([P, N // 16], U16, name="offsets")
+        nc.sync.dma_start(offsets[:], offs)
+        vloc_bc = held.tile([P, N], F32, name="vloc_bc")
+        nc.scalar.dma_start(vloc_bc[:], v_loc.rearrange("o n -> (o n)").partition_broadcast(P))
+
+        w_mem_sb = held.tile([P, CB], BF16, name="w_mem_sb")
+        w_vec_sb = held.tile([P, CB], BF16, name="w_vec_sb")
+        b_lin_sb = held.tile([P, CB], F32, name="b_lin_sb")
+        b_out_sb = held.tile([P, 1], F32, name="b_out_sb")
+        with nc.allow_non_contiguous_dma(reason="one value to a partition"):
+            nc.scalar.dma_start(w_mem_sb[:], w_mem.rearrange("(a p) o -> p (a o)", p=P))
+            nc.scalar.dma_start(w_vec_sb[:], w_vec.rearrange("(a p) o -> p (a o)", p=P))
+            nc.scalar.dma_start(b_lin_sb[:], b_lin.rearrange("(a p) o -> p (a o)", p=P))
+            nc.scalar.dma_start(b_out_sb[:], b_out)
+
+        identity = held.tile([P, P], F32, name="identity")
+        make_identity(nc, identity[:])
+
+        memory = [held.tile([P, L, C], F32, name=f"memory{s}") for s in range(QB)]
+        e_parts = psum.tile([P, CB, QB * L], F32, name="e_parts", bufs=1)
+
+        emb_blocks = emb.rearrange("(a p) s -> a p s", p=P)
+        for a in range(CB):
+            window = windows.tile([P, S], F32, name="window")
+            nc.sync.dma_start(window[:], emb_blocks[a])
+            for s in range(QB):
+                ext = picked.tile([P, NB], F32, name="ext")
+                nc.vector.tensor_tensor(
+                    ext[:],
+                    window[:].indirect(offsets[:, s * NB // 16 : (s + 1) * NB // 16]),
+                    vloc_bc[:, s * NB : (s + 1) * NB],
+                    MULT,
+                )
+                ext_bf = picked.tile([P, NB], BF16, name="ext_bf")
+                nc.scalar.copy(ext_bf[:], ext[:])
+                for g in range(L // FLIPS):
+                    flipped = psum.tile([P, FLIPS, P], F32, name="flipped")
+                    for i in range(FLIPS):
+                        nc.tensor.transpose(flipped[:, i, :], ext[:, g * FLIPS + i : NB : L], identity[:])
+                    nc.scalar.copy(
+                        memory[s][:, g * FLIPS : (g + 1) * FLIPS, a * P : (a + 1) * P], flipped[:]
+                    )
+                for t in range(L):
+                    nc.tensor.matmul(
+                        e_parts[:, a, s * L + t : s * L + t + 1],
+                        lhsT=ext_bf[:, t:NB:L],
+                        rhs=w_mem_sb[:, a : a + 1],
+                        start=True,
+                        stop=True,
+                    )
+
+        aspect_sb = held.tile([P, CB, Q], F32, name="aspect_sb")
+        nc.sync.dma_start(aspect_sb[:], aspect.rearrange("(a p) q -> p a q", p=P))
+        w_lin_sb = held.tile([P, CB, C], BF16, name="w_lin_sb")
+        nc.sync.dma_start(w_lin_sb[:], w_lin.rearrange("(a p) d -> p a d", p=P))
+        w_out_sb = held.tile([P, CB, K], BF16, name="w_out_sb")
+        nc.sync.dma_start(w_out_sb[:], w_out.rearrange("(a p) k -> p a k", p=P))
+
+        e_sum = held.tile([P, QB * L], F32, name="e_sum")
+        nc.vector.tensor_reduce(
+            out=e_sum[:], in_=e_parts[:].rearrange("p a j -> p j a"), axis=mybir.AxisListType.X, op=ADD
+        )
+        e_biased = held.tile([P, QB * L], F32, name="e_biased")
+        nc.vector.tensor_scalar_add(e_biased[:], e_sum[:], B_ATT)
+
+        def prepare(s, vec):
+            u_ps = psum.tile([P, 1], F32, name="u_ps", tag="narrow", bufs=1)
+            for a in range(CB):
+                nc.tensor.matmul(
+                    u_ps[:], lhsT=vec[:, a, :], rhs=w_vec_sb[:, a : a + 1], start=(a == 0), stop=(a == CB - 1)
+                )
+            lin = [psum.tile([P, BANK], F32, name=f"lin{half}") for half in range(HALVES)]
+            for half in range(HALVES):
+                for a in range(CB):
+                    nc.tensor.matmul(
+                        lin[half][:],
+                        lhsT=vec[:, a, :],
+                        rhs=w_lin_sb[:, a, half * BANK : (half + 1) * BANK],
+                        start=(a == 0),
+                        stop=(a == CB - 1),
+                    )
+            u_sb = small.tile([P, 1], F32, name="u_sb")
+            nc.scalar.copy(u_sb[:], u_ps[:])
+            score = small.tile([P, L], F32, name="score")
+            nc.scalar.activation(score[:], e_biased[:, s * L : (s + 1) * L], ACT.Tanh, bias=u_sb[:, 0:1])
+            weight = small.tile([P, L], F32, name="weight")
+            total = small.tile([P, 1], F32, name="total")
+            nc.scalar.activation(weight[:], score[:], ACT.Exp, accum_out=total[:])
+            first = sums.tile([P, C], F32, name="acc")
+            nc.scalar.activation(first[:], memory[s][:, 0, :], ACT.Identity, scale=weight[:, 0:1])
+            return weight, total, first, lin
+
+        def attend(s, weight, total, acc, lin):
+            for t in range(1, L):
+                longer = sums.tile([P, C], F32, name="acc")
+                nc.vector.scalar_tensor_tensor(
+                    longer[:], in0=memory[s][:, t, :], scalar=weight[:, t : t + 1], in1=acc[:], op0=MULT, op1=ADD
+                )
+                acc = longer
+            inverse = small.tile([P, 1], F32, name="inverse")
+            nc.vector.reciprocal(inverse[:], total[:])
+            vec_rows = rows.tile([P, C], F32, name="vec_rows")
+            for half in range(HALVES):
+                cols = slice(half * BANK, (half + 1) * BANK)
+                nc.vector.scalar_tensor_tensor(
+                    vec_rows[:, cols], in0=acc[:, cols], scalar=inverse[:, 0:1], in1=lin[half][:], op0=MULT, op1=ADD
+                )
+            return vec_rows
+
+        def flip_back(vec_rows):
+            vec = vecs.tile([P, CB, P], BF16, name="vec")
+            for half in range(HALVES):
+                flipped = psum.tile([P, FLIPS, P], F32, name="flipped")
+                for i in range(FLIPS):
+                    a = half * FLIPS + i
+                    nc.tensor.transpose(flipped[:, i, :], vec_rows[:, a * P : (a + 1) * P], identity[:])
+                for i in range(FLIPS):
+                    a = half * FLIPS + i
+                    nc.scalar.activation(vec[:, a, :], flipped[:, i, :], ACT.Identity, bias=b_lin_sb[:, a : a + 1])
+            return vec
+
+        def classify(s, vec):
+            out_ps = psum.tile([P, P], F32, name="out_ps", tag="narrow", bufs=1)
+            for a in range(CB):
+                nc.tensor.matmul(
+                    out_ps[:], lhsT=w_out_sb[:, a, :], rhs=vec[:, a, :], start=(a == 0), stop=(a == CB - 1)
+                )
+            out_sb = rows.tile([P, P], F32, name="out_sb")
+            nc.scalar.activation(out_sb[:], out_ps[:], ACT.Identity, bias=b_out_sb[:, 0:1])
+            nc.sync.dma_start(out[:, s * P : (s + 1) * P], out_sb[:])
+
+        ready = []
+        for s in range(QB):
+            vec = vecs.tile([P, CB, P], BF16, name="vec")
+            nc.scalar.copy(vec[:], aspect_sb[:, :, s * P : (s + 1) * P])
+            ready.append(prepare(s, vec))
+        for h in range(HOPS):
+            for s in range(QB):
+                vec = flip_back(attend(s, *ready[s]))
+                if h < HOPS - 1:
+                    ready[s] = prepare(s, vec)
+                else:
+                    classify(s, vec)

@@ -14,6 +14,7 @@ NB = N // QB
 BANK = 512
 FLIPS = BANK // P
 HALVES = C // BANK
+SUMS = 2
 
 FLOPS = 2 * C * N + HOPS * (2 * C * Q + 2 * C * C * Q + 2 * C * N) + 2 * C * K * Q
 
@@ -28,8 +29,7 @@ def tile_memnet_b_kernel(
         tc.tile_pool(name="picked", bufs=4) as picked,
         tc.tile_pool(name="vecs", bufs=2 * QB) as vecs,
         tc.tile_pool(name="small", bufs=2 * QB) as small,
-        tc.tile_pool(name="sums", bufs=3) as sums,
-        tc.tile_pool(name="rows", bufs=2) as rows,
+        tc.tile_pool(name="rows", bufs=3) as rows,
         tc.psum_pool(name="psum", bufs=2) as psum,
     ):
         offsets = held.tile([P, N // 16], U16, name="offsets")
@@ -51,6 +51,7 @@ def tile_memnet_b_kernel(
         make_identity(nc, identity[:])
 
         memory = [held.tile([P, L, C], F32, name=f"memory{s}") for s in range(QB)]
+        acc = [[held.tile([P, C], F32, name=f"acc{s}{k}") for k in range(SUMS)] for s in range(QB)]
         e_parts = psum.tile([P, CB, QB * L], F32, name="e_parts", bufs=1)
 
         emb_blocks = emb.rearrange("(a p) s -> a p s", p=P)
@@ -120,25 +121,38 @@ def tile_memnet_b_kernel(
             weight = small.tile([P, L], F32, name="weight")
             total = small.tile([P, 1], F32, name="total")
             nc.scalar.activation(weight[:], score[:], ACT.Exp, accum_out=total[:])
-            first = sums.tile([P, C], F32, name="acc")
-            nc.scalar.activation(first[:], memory[s][:, 0, :], ACT.Identity, scale=weight[:, 0:1])
-            return weight, total, first, lin
+            for k in range(SUMS):
+                t = k * (L // SUMS)
+                nc.scalar.activation(acc[s][k][:], memory[s][:, t, :], ACT.Identity, scale=weight[:, t : t + 1])
+            return weight, total, lin
 
-        def attend(s, weight, total, acc, lin):
-            for t in range(1, L):
-                longer = sums.tile([P, C], F32, name="acc")
-                nc.vector.scalar_tensor_tensor(
-                    longer[:], in0=memory[s][:, t, :], scalar=weight[:, t : t + 1], in1=acc[:], op0=MULT, op1=ADD
-                )
-                acc = longer
+        def attend(s, weight, total, lin):
             inverse = small.tile([P, 1], F32, name="inverse")
             nc.vector.reciprocal(inverse[:], total[:])
-            vec_rows = rows.tile([P, C], F32, name="vec_rows")
-            for half in range(HALVES):
-                cols = slice(half * BANK, (half + 1) * BANK)
-                nc.vector.scalar_tensor_tensor(
-                    vec_rows[:, cols], in0=acc[:, cols], scalar=inverse[:, 0:1], in1=lin[half][:], op0=MULT, op1=ADD
-                )
+            for i in range(1, L // SUMS):
+                for k in range(SUMS):
+                    t = k * (L // SUMS) + i
+                    nc.vector.scalar_tensor_tensor(
+                        acc[s][k][:],
+                        in0=memory[s][:, t, :],
+                        scalar=weight[:, t : t + 1],
+                        in1=acc[s][k][:],
+                        op0=MULT,
+                        op1=ADD,
+                    )
+            vec_rows = lin
+            for k in range(SUMS):
+                added = [rows.tile([P, BANK], F32, name=f"vec_rows{half}") for half in range(HALVES)]
+                for half in range(HALVES):
+                    nc.vector.scalar_tensor_tensor(
+                        added[half][:],
+                        in0=acc[s][k][:, half * BANK : (half + 1) * BANK],
+                        scalar=inverse[:, 0:1],
+                        in1=vec_rows[half][:],
+                        op0=MULT,
+                        op1=ADD,
+                    )
+                vec_rows = added
             return vec_rows
 
         def flip_back(vec_rows):
@@ -146,8 +160,7 @@ def tile_memnet_b_kernel(
             for half in range(HALVES):
                 flipped = psum.tile([P, FLIPS, P], F32, name="flipped")
                 for i in range(FLIPS):
-                    a = half * FLIPS + i
-                    nc.tensor.transpose(flipped[:, i, :], vec_rows[:, a * P : (a + 1) * P], identity[:])
+                    nc.tensor.transpose(flipped[:, i, :], vec_rows[half][:, i * P : (i + 1) * P], identity[:])
                 for i in range(FLIPS):
                     a = half * FLIPS + i
                     nc.scalar.activation(vec[:, a, :], flipped[:, i, :], ACT.Identity, bias=b_lin_sb[:, a : a + 1])

@@ -6,7 +6,7 @@ MULT, ADD = mybir.AluOpType.mult, mybir.AluOpType.add
 ACT = mybir.ActivationFunctionType
 
 P = 128
-C, S, N, Q, L, K, HOPS = 1024, 4096, 2048, 256, 8, 128, 6
+C, W, N, Q, L, K, HOPS = 1024, 4096, 2048, 256, 8, 128, 6
 B_ATT = 0.5
 CB = C // P
 QB = Q // P
@@ -29,7 +29,7 @@ def tile_memnet_b_kernel(
         tc.tile_pool(name="picked", bufs=4) as picked,
         tc.tile_pool(name="vecs", bufs=2 * QB) as vecs,
         tc.tile_pool(name="small", bufs=2 * QB) as small,
-        tc.tile_pool(name="rows", bufs=3) as rows,
+        tc.tile_pool(name="results", bufs=QB) as results,
         tc.psum_pool(name="psum", bufs=2) as psum,
     ):
         offsets = held.tile([P, N // 16], U16, name="offsets")
@@ -51,12 +51,16 @@ def tile_memnet_b_kernel(
         make_identity(nc, identity[:])
 
         memory = [held.tile([P, L, C], F32, name=f"memory{s}") for s in range(QB)]
-        acc = [[held.tile([P, C], F32, name=f"acc{s}{k}") for k in range(SUMS)] for s in range(QB)]
+        part = [[held.tile([P, C], F32, name=f"part{s}{k}") for k in range(SUMS + 1)] for s in range(QB)]
+        turned = [
+            [psum.tile([P, FLIPS, P], F32, name=f"turned{s}{half}", bufs=1) for half in range(HALVES)]
+            for s in range(QB)
+        ]
         e_parts = psum.tile([P, CB, QB * L], F32, name="e_parts", bufs=1)
 
-        emb_blocks = emb.rearrange("(a p) s -> a p s", p=P)
+        emb_blocks = emb.rearrange("(a p) w -> a p w", p=P)
         for a in range(CB):
-            window = windows.tile([P, S], F32, name="window")
+            window = windows.tile([P, W], F32, name="window")
             nc.sync.dma_start(window[:], emb_blocks[a])
             for s in range(QB):
                 ext = picked.tile([P, NB], F32, name="ext")
@@ -98,72 +102,75 @@ def tile_memnet_b_kernel(
         e_biased = held.tile([P, QB * L], F32, name="e_biased")
         nc.vector.tensor_scalar_add(e_biased[:], e_sum[:], B_ATT)
 
-        def prepare(s, vec):
+        def linear(s, vec, half):
+            for i in range(FLIPS):
+                d = half * FLIPS + i
+                for a in range(CB):
+                    nc.tensor.matmul(
+                        turned[s][half][:, i, :],
+                        lhsT=w_lin_sb[:, a, d * P : (d + 1) * P],
+                        rhs=vec[:, a, :],
+                        start=(i == 0 and a == 0),
+                        stop=False,
+                    )
+
+        def weigh(s, vec):
             u_ps = psum.tile([P, 1], F32, name="u_ps", tag="narrow", bufs=1)
             for a in range(CB):
                 nc.tensor.matmul(
                     u_ps[:], lhsT=vec[:, a, :], rhs=w_vec_sb[:, a : a + 1], start=(a == 0), stop=(a == CB - 1)
                 )
-            lin = [psum.tile([P, BANK], F32, name=f"lin{half}") for half in range(HALVES)]
-            for half in range(HALVES):
-                for a in range(CB):
-                    nc.tensor.matmul(
-                        lin[half][:],
-                        lhsT=vec[:, a, :],
-                        rhs=w_lin_sb[:, a, half * BANK : (half + 1) * BANK],
-                        start=(a == 0),
-                        stop=(a == CB - 1),
-                    )
             u_sb = small.tile([P, 1], F32, name="u_sb")
             nc.scalar.copy(u_sb[:], u_ps[:])
             score = small.tile([P, L], F32, name="score")
             nc.scalar.activation(score[:], e_biased[:, s * L : (s + 1) * L], ACT.Tanh, bias=u_sb[:, 0:1])
-            weight = small.tile([P, L], F32, name="weight")
+            grown = small.tile([P, L], F32, name="grown")
             total = small.tile([P, 1], F32, name="total")
-            nc.scalar.activation(weight[:], score[:], ACT.Exp, accum_out=total[:])
-            for k in range(SUMS):
-                t = k * (L // SUMS)
-                nc.scalar.activation(acc[s][k][:], memory[s][:, t, :], ACT.Identity, scale=weight[:, t : t + 1])
-            return weight, total, lin
-
-        def attend(s, weight, total, lin):
+            nc.scalar.activation(grown[:], score[:], ACT.Exp, accum_out=total[:])
             inverse = small.tile([P, 1], F32, name="inverse")
             nc.vector.reciprocal(inverse[:], total[:])
-            for i in range(1, L // SUMS):
-                for k in range(SUMS):
-                    t = k * (L // SUMS) + i
-                    nc.vector.scalar_tensor_tensor(
-                        acc[s][k][:],
-                        in0=memory[s][:, t, :],
-                        scalar=weight[:, t : t + 1],
-                        in1=acc[s][k][:],
-                        op0=MULT,
-                        op1=ADD,
-                    )
-            vec_rows = lin
-            for k in range(SUMS):
-                added = [rows.tile([P, BANK], F32, name=f"vec_rows{half}") for half in range(HALVES)]
-                for half in range(HALVES):
-                    nc.vector.scalar_tensor_tensor(
-                        added[half][:],
-                        in0=acc[s][k][:, half * BANK : (half + 1) * BANK],
-                        scalar=inverse[:, 0:1],
-                        in1=vec_rows[half][:],
-                        op0=MULT,
-                        op1=ADD,
-                    )
-                vec_rows = added
-            return vec_rows
+            alpha = small.tile([P, L], F32, name="alpha")
+            nc.scalar.activation(alpha[:], grown[:], ACT.Identity, scale=inverse[:, 0:1])
+            nc.scalar.activation(part[s][SUMS][:], memory[s][:, 0, :], ACT.Identity, scale=alpha[:, 0:1])
+            return alpha
 
-        def flip_back(vec_rows):
+        def attend(s, alpha):
+            for t in range(1, L):
+                k = t % SUMS
+                if t <= SUMS:
+                    nc.vector.tensor_scalar_mul(part[s][k][:], memory[s][:, t, :], alpha[:, t : t + 1])
+                else:
+                    nc.vector.scalar_tensor_tensor(
+                        part[s][k][:],
+                        in0=memory[s][:, t, :],
+                        scalar=alpha[:, t : t + 1],
+                        in1=part[s][k][:],
+                        op0=MULT,
+                        op1=ADD,
+                    )
+
+        def add_flipped(s):
+            for k in (SUMS, (L - 2) % SUMS, (L - 1) % SUMS):
+                for half in range(HALVES):
+                    for i in range(FLIPS):
+                        d = half * FLIPS + i
+                        nc.tensor.matmul(
+                            turned[s][half][:, i, :],
+                            lhsT=part[s][k][:, d * P : (d + 1) * P],
+                            rhs=identity[:],
+                            is_transpose=True,
+                            start=False,
+                            stop=(k == (L - 1) % SUMS and i == FLIPS - 1),
+                        )
+
+        def round_off(s):
             vec = vecs.tile([P, CB, P], BF16, name="vec")
             for half in range(HALVES):
-                flipped = psum.tile([P, FLIPS, P], F32, name="flipped")
                 for i in range(FLIPS):
-                    nc.tensor.transpose(flipped[:, i, :], vec_rows[half][:, i * P : (i + 1) * P], identity[:])
-                for i in range(FLIPS):
-                    a = half * FLIPS + i
-                    nc.scalar.activation(vec[:, a, :], flipped[:, i, :], ACT.Identity, bias=b_lin_sb[:, a : a + 1])
+                    d = half * FLIPS + i
+                    nc.scalar.activation(
+                        vec[:, d, :], turned[s][half][:, i, :], ACT.Identity, bias=b_lin_sb[:, d : d + 1]
+                    )
             return vec
 
         def classify(s, vec):
@@ -172,19 +179,29 @@ def tile_memnet_b_kernel(
                 nc.tensor.matmul(
                     out_ps[:], lhsT=w_out_sb[:, a, :], rhs=vec[:, a, :], start=(a == 0), stop=(a == CB - 1)
                 )
-            out_sb = rows.tile([P, P], F32, name="out_sb")
+            out_sb = results.tile([P, P], F32, name="out_sb")
             nc.scalar.activation(out_sb[:], out_ps[:], ACT.Identity, bias=b_out_sb[:, 0:1])
             nc.sync.dma_start(out[:, s * P : (s + 1) * P], out_sb[:])
 
-        ready = []
+        alphas = []
         for s in range(QB):
             vec = vecs.tile([P, CB, P], BF16, name="vec")
             nc.scalar.copy(vec[:], aspect_sb[:, :, s * P : (s + 1) * P])
-            ready.append(prepare(s, vec))
+            alphas.append(weigh(s, vec))
+            for half in range(HALVES):
+                linear(s, vec, half)
+        late = None
         for h in range(HOPS):
             for s in range(QB):
-                vec = flip_back(attend(s, *ready[s]))
+                attend(s, alphas[s])
+                add_flipped(s)
+                if late is not None:
+                    linear(late[0], late[1], 1)
+                vec = round_off(s)
                 if h < HOPS - 1:
-                    ready[s] = prepare(s, vec)
+                    alphas[s] = weigh(s, vec)
+                    linear(s, vec, 0)
+                    late = (s, vec)
                 else:
                     classify(s, vec)
+                    late = None

@@ -14,6 +14,7 @@ NB = N // QB
 BANK = 512
 FLIPS = BANK // P
 HALVES = C // BANK
+ROWS = 32
 SUMS = 2
 
 FLOPS = 2 * C * N + HOPS * (2 * C * Q + 2 * C * C * Q + 2 * C * N) + 2 * C * K * Q
@@ -34,21 +35,40 @@ def tile_memnet_b_kernel(
     ):
         offsets = held.tile([P, N // 16], U16, name="offsets")
         nc.sync.dma_start(offsets[:], offs)
-        vloc_bc = held.tile([P, N], F32, name="vloc_bc")
-        nc.scalar.dma_start(vloc_bc[:], v_loc.rearrange("o n -> (o n)").partition_broadcast(P))
-
-        w_mem_sb = held.tile([P, CB], BF16, name="w_mem_sb")
-        w_vec_sb = held.tile([P, CB], BF16, name="w_vec_sb")
-        b_lin_sb = held.tile([P, CB], F32, name="b_lin_sb")
-        b_out_sb = held.tile([P, 1], F32, name="b_out_sb")
-        with nc.allow_non_contiguous_dma(reason="one value to a partition"):
-            nc.scalar.dma_start(w_mem_sb[:], w_mem.rearrange("(a p) o -> p (a o)", p=P))
-            nc.scalar.dma_start(w_vec_sb[:], w_vec.rearrange("(a p) o -> p (a o)", p=P))
-            nc.scalar.dma_start(b_lin_sb[:], b_lin.rearrange("(a p) o -> p (a o)", p=P))
-            nc.scalar.dma_start(b_out_sb[:], b_out)
-
         identity = held.tile([P, P], F32, name="identity")
         make_identity(nc, identity[:])
+
+        vloc_rows = held.tile([ROWS, N], F32, name="vloc_rows")
+        nc.scalar.dma_start(vloc_rows[:], v_loc.rearrange("o n -> (o n)").partition_broadcast(ROWS))
+        row0 = held.tile([ROWS, P], F32, name="row0")
+        nc.vector.memset(row0[:], 0.0)
+        nc.vector.memset(row0[0:1, :], 1.0)
+        vloc_bc = held.tile([P, N], F32, name="vloc_bc")
+        for b in range(N // BANK):
+            spread = psum.tile([P, BANK], F32, name="spread", tag="flipped")
+            nc.tensor.matmul(spread[:], lhsT=row0[:], rhs=vloc_rows[:, b * BANK : (b + 1) * BANK], start=True, stop=True)
+            nc.scalar.copy(vloc_bc[:, b * BANK : (b + 1) * BANK], spread[:])
+
+        w_rows = held.tile([ROWS, P], BF16, name="w_rows")
+        nc.vector.memset(w_rows[:], 0.0)
+        nc.scalar.dma_start(w_rows[0:CB, :], w_mem.rearrange("(a p) o -> a (p o)", p=P))
+        nc.scalar.dma_start(w_rows[CB : 2 * CB, :], w_vec.rearrange("(a p) o -> a (p o)", p=P))
+        b_rows = held.tile([ROWS, P], F32, name="b_rows")
+        nc.vector.memset(b_rows[:], 0.0)
+        nc.scalar.dma_start(b_rows[0:CB, :], b_lin.rearrange("(a p) o -> a (p o)", p=P))
+        nc.scalar.dma_start(b_rows[CB : CB + 1, :], b_out.rearrange("k o -> o k"))
+        identity_bf = held.tile([ROWS, 2 * CB], BF16, name="identity_bf")
+        nc.vector.tensor_copy(identity_bf[:], identity[0:ROWS, 0 : 2 * CB])
+        w_ps = psum.tile([P, 2 * CB], F32, name="w_ps", tag="narrow", bufs=1)
+        nc.tensor.matmul(w_ps[:], lhsT=w_rows[:], rhs=identity_bf[:], start=True, stop=True)
+        w_cols = held.tile([P, 2 * CB], BF16, name="w_cols")
+        nc.vector.tensor_copy(w_cols[:], w_ps[:])
+        b_ps = psum.tile([P, CB + 1], F32, name="b_ps", tag="narrow", bufs=1)
+        nc.tensor.matmul(b_ps[:], lhsT=b_rows[:], rhs=identity[0:ROWS, 0 : CB + 1], start=True, stop=True)
+        b_cols = held.tile([P, CB + 1], F32, name="b_cols")
+        nc.vector.tensor_copy(b_cols[:], b_ps[:])
+        w_mem_sb, w_vec_sb = w_cols[:, 0:CB], w_cols[:, CB : 2 * CB]
+        b_lin_sb, b_out_sb = b_cols[:, 0:CB], b_cols[:, CB : CB + 1]
 
         memory = [held.tile([P, L, C], F32, name=f"memory{s}") for s in range(QB)]
         part = [[held.tile([P, C], F32, name=f"part{s}{k}") for k in range(SUMS + 1)] for s in range(QB)]

@@ -15,7 +15,8 @@ BANK = 512
 FLIPS = BANK // P
 HALVES = C // BANK
 ROWS = 32
-SUMS = 2
+SCALAR_WORDS = 2
+LAST = 2
 
 FLOPS = 2 * C * N + HOPS * (2 * C * Q + 2 * C * C * Q + 2 * C * N) + 2 * C * K * Q
 
@@ -38,32 +39,38 @@ def tile_memnet_b_kernel(
         identity = held.tile([P, P], F32, name="identity")
         make_identity(nc, identity[:])
 
-        vloc_rows = held.tile([ROWS, N], F32, name="vloc_rows")
-        nc.scalar.dma_start(vloc_rows[:], v_loc.rearrange("o n -> (o n)").partition_broadcast(ROWS))
-        row0 = held.tile([ROWS, P], F32, name="row0")
-        nc.vector.memset(row0[:], 0.0)
-        nc.vector.memset(row0[0:1, :], 1.0)
+        vloc_rows = held.tile([ROWS, P], F32, name="vloc_rows")
+        for copy in range(ROWS * P // N):
+            nc.sync.dma_start(
+                vloc_rows[copy * N // P : (copy + 1) * N // P, :], v_loc.rearrange("o (r p) -> (o r) p", p=P)
+            )
+        vloc_ps = psum.tile([P, N // P], F32, name="vloc_ps", tag="narrow0", bufs=1)
+        nc.tensor.matmul(vloc_ps[:], lhsT=vloc_rows[:], rhs=identity[0:ROWS, 0 : N // P], start=True, stop=True)
+        vloc_cols = held.tile([P, N // P], F32, name="vloc_cols")
+        nc.vector.tensor_copy(vloc_cols[:], vloc_ps[:])
         vloc_bc = held.tile([P, N], F32, name="vloc_bc")
         for b in range(N // BANK):
-            spread = psum.tile([P, BANK], F32, name="spread", tag="flipped")
-            nc.tensor.matmul(spread[:], lhsT=row0[:], rhs=vloc_rows[:, b * BANK : (b + 1) * BANK], start=True, stop=True)
+            spread = psum.tile([P, FLIPS, P], F32, name="spread", tag="flipped")
+            for i in range(FLIPS):
+                r = b * FLIPS + i
+                nc.tensor.transpose(spread[:, i, :], vloc_cols[:, r : r + 1].to_broadcast([P, P]), identity[:])
             nc.scalar.copy(vloc_bc[:, b * BANK : (b + 1) * BANK], spread[:])
 
         w_rows = held.tile([ROWS, P], BF16, name="w_rows")
         nc.vector.memset(w_rows[:], 0.0)
-        nc.scalar.dma_start(w_rows[0:CB, :], w_mem.rearrange("(a p) o -> a (p o)", p=P))
-        nc.scalar.dma_start(w_rows[CB : 2 * CB, :], w_vec.rearrange("(a p) o -> a (p o)", p=P))
+        nc.sync.dma_start(w_rows[0:CB, :], w_mem.rearrange("(a p) o -> a (p o)", p=P))
+        nc.sync.dma_start(w_rows[CB : 2 * CB, :], w_vec.rearrange("(a p) o -> a (p o)", p=P))
         b_rows = held.tile([ROWS, P], F32, name="b_rows")
         nc.vector.memset(b_rows[:], 0.0)
-        nc.scalar.dma_start(b_rows[0:CB, :], b_lin.rearrange("(a p) o -> a (p o)", p=P))
-        nc.scalar.dma_start(b_rows[CB : CB + 1, :], b_out.rearrange("k o -> o k"))
+        nc.sync.dma_start(b_rows[0:CB, :], b_lin.rearrange("(a p) o -> a (p o)", p=P))
+        nc.sync.dma_start(b_rows[CB : CB + 1, :], b_out.rearrange("k o -> o k"))
         identity_bf = held.tile([ROWS, 2 * CB], BF16, name="identity_bf")
         nc.vector.tensor_copy(identity_bf[:], identity[0:ROWS, 0 : 2 * CB])
-        w_ps = psum.tile([P, 2 * CB], F32, name="w_ps", tag="narrow", bufs=1)
+        w_ps = psum.tile([P, 2 * CB], F32, name="w_ps", tag="narrow0", bufs=1)
         nc.tensor.matmul(w_ps[:], lhsT=w_rows[:], rhs=identity_bf[:], start=True, stop=True)
         w_cols = held.tile([P, 2 * CB], BF16, name="w_cols")
         nc.vector.tensor_copy(w_cols[:], w_ps[:])
-        b_ps = psum.tile([P, CB + 1], F32, name="b_ps", tag="narrow", bufs=1)
+        b_ps = psum.tile([P, CB + 1], F32, name="b_ps", tag="narrow1", bufs=1)
         nc.tensor.matmul(b_ps[:], lhsT=b_rows[:], rhs=identity[0:ROWS, 0 : CB + 1], start=True, stop=True)
         b_cols = held.tile([P, CB + 1], F32, name="b_cols")
         nc.vector.tensor_copy(b_cols[:], b_ps[:])
@@ -71,79 +78,82 @@ def tile_memnet_b_kernel(
         b_lin_sb, b_out_sb = b_cols[:, 0:CB], b_cols[:, CB : CB + 1]
 
         memory = [held.tile([P, L, C], F32, name=f"memory{s}") for s in range(QB)]
-        part = [[held.tile([P, C], F32, name=f"part{s}{k}") for k in range(SUMS + 1)] for s in range(QB)]
-        turned = [
-            [psum.tile([P, FLIPS, P], F32, name=f"turned{s}{half}", bufs=1) for half in range(HALVES)]
-            for s in range(QB)
-        ]
-        e_parts = psum.tile([P, CB, QB * L], F32, name="e_parts", bufs=1)
+        part = [[held.tile([P, C], F32, name=f"part{s}{k}") for k in range(1 + SCALAR_WORDS)] for s in range(QB)]
+        e_ps = [psum.tile([P, L], F32, name=f"e_ps{s}", bufs=1) for s in range(QB)]
 
         emb_blocks = emb.rearrange("(a p) w -> a p w", p=P)
-        for a in range(CB):
+
+        def load(a):
             window = windows.tile([P, W], F32, name="window")
             nc.sync.dma_start(window[:], emb_blocks[a])
-            for s in range(QB):
-                ext = picked.tile([P, NB], F32, name="ext")
-                nc.vector.tensor_tensor(
-                    ext[:],
-                    window[:].indirect(offsets[:, s * NB // 16 : (s + 1) * NB // 16]),
-                    vloc_bc[:, s * NB : (s + 1) * NB],
-                    MULT,
+            return window
+
+        def look_up(window, s):
+            ext = picked.tile([P, NB], F32, name="ext")
+            nc.vector.tensor_tensor(
+                ext[:],
+                window[:].indirect(offsets[:, s * NB // 16 : (s + 1) * NB // 16]),
+                vloc_bc[:, s * NB : (s + 1) * NB],
+                MULT,
+            )
+            return ext
+
+        def remember(a, s, ext):
+            ext_bf = picked.tile([P, NB], BF16, name="ext_bf")
+            nc.scalar.copy(ext_bf[:], ext[:])
+            for g in range(L // FLIPS):
+                flipped = psum.tile([P, FLIPS, P], F32, name="flipped")
+                for i in range(FLIPS):
+                    nc.tensor.transpose(flipped[:, i, :], ext[:, g * FLIPS + i : NB : L], identity[:])
+                nc.scalar.copy(memory[s][:, g * FLIPS : (g + 1) * FLIPS, a * P : (a + 1) * P], flipped[:])
+            for t in range(L):
+                nc.tensor.matmul(
+                    e_ps[s][:, t : t + 1],
+                    lhsT=ext_bf[:, t:NB:L],
+                    rhs=w_mem_sb[:, a : a + 1],
+                    start=(a == 0 and t == 0),
+                    stop=(a == CB - 1 and t == L - 1),
                 )
-                ext_bf = picked.tile([P, NB], BF16, name="ext_bf")
-                nc.scalar.copy(ext_bf[:], ext[:])
-                for g in range(L // FLIPS):
-                    flipped = psum.tile([P, FLIPS, P], F32, name="flipped")
-                    for i in range(FLIPS):
-                        nc.tensor.transpose(flipped[:, i, :], ext[:, g * FLIPS + i : NB : L], identity[:])
-                    nc.scalar.copy(
-                        memory[s][:, g * FLIPS : (g + 1) * FLIPS, a * P : (a + 1) * P], flipped[:]
-                    )
-                for t in range(L):
-                    nc.tensor.matmul(
-                        e_parts[:, a, s * L + t : s * L + t + 1],
-                        lhsT=ext_bf[:, t:NB:L],
-                        rhs=w_mem_sb[:, a : a + 1],
-                        start=True,
-                        stop=True,
-                    )
+
+        for a in range(CB - LAST):
+            window = load(a)
+            for s in range(QB):
+                remember(a, s, look_up(window, s))
+        last_windows = [load(a) for a in range(CB - LAST, CB)]
 
         aspect_sb = held.tile([P, CB, Q], F32, name="aspect_sb")
         nc.sync.dma_start(aspect_sb[:], aspect.rearrange("(a p) q -> p a q", p=P))
-        w_lin_sb = held.tile([P, CB, C], BF16, name="w_lin_sb")
-        nc.sync.dma_start(w_lin_sb[:], w_lin.rearrange("(a p) d -> p a d", p=P))
+        w_lin_sb = [held.tile([P, CB, BANK], BF16, name=f"w_lin_sb{half}") for half in range(HALVES)]
+        w_lin_halves = w_lin.rearrange("(a p) (half d) -> half p a d", p=P, half=HALVES)
+        for half in range(HALVES):
+            nc.sync.dma_start(w_lin_sb[half][:], w_lin_halves[half])
         w_out_sb = held.tile([P, CB, K], BF16, name="w_out_sb")
         nc.sync.dma_start(w_out_sb[:], w_out.rearrange("(a p) k -> p a k", p=P))
 
-        e_sum = held.tile([P, QB * L], F32, name="e_sum")
-        nc.vector.tensor_reduce(
-            out=e_sum[:], in_=e_parts[:].rearrange("p a j -> p j a"), axis=mybir.AxisListType.X, op=ADD
-        )
-        e_biased = held.tile([P, QB * L], F32, name="e_biased")
-        nc.vector.tensor_scalar_add(e_biased[:], e_sum[:], B_ATT)
-
         def linear(s, vec, half):
             for i in range(FLIPS):
-                d = half * FLIPS + i
                 for a in range(CB):
                     nc.tensor.matmul(
                         turned[s][half][:, i, :],
-                        lhsT=w_lin_sb[:, a, d * P : (d + 1) * P],
+                        lhsT=w_lin_sb[half][:, a, i * P : (i + 1) * P],
                         rhs=vec[:, a, :],
                         start=(i == 0 and a == 0),
                         stop=False,
                     )
 
-        def weigh(s, vec):
-            u_ps = psum.tile([P, 1], F32, name="u_ps", tag="narrow", bufs=1)
+        def project(s, vec):
+            u_ps = psum.tile([P, 1], F32, name="u_ps", tag=f"narrow{s}", bufs=1)
             for a in range(CB):
                 nc.tensor.matmul(
                     u_ps[:], lhsT=vec[:, a, :], rhs=w_vec_sb[:, a : a + 1], start=(a == 0), stop=(a == CB - 1)
                 )
             u_sb = small.tile([P, 1], F32, name="u_sb")
-            nc.scalar.copy(u_sb[:], u_ps[:])
+            nc.scalar.activation(u_sb[:], u_ps[:], ACT.Identity, bias=B_ATT)
+            return u_sb
+
+        def weigh(s, u_sb):
             score = small.tile([P, L], F32, name="score")
-            nc.scalar.activation(score[:], e_biased[:, s * L : (s + 1) * L], ACT.Tanh, bias=u_sb[:, 0:1])
+            nc.scalar.activation(score[:], e_ps[s][:], ACT.Tanh, bias=u_sb[:, 0:1])
             grown = small.tile([P, L], F32, name="grown")
             total = small.tile([P, 1], F32, name="total")
             nc.scalar.activation(grown[:], score[:], ACT.Exp, accum_out=total[:])
@@ -151,26 +161,28 @@ def tile_memnet_b_kernel(
             nc.vector.reciprocal(inverse[:], total[:])
             alpha = small.tile([P, L], F32, name="alpha")
             nc.scalar.activation(alpha[:], grown[:], ACT.Identity, scale=inverse[:, 0:1])
-            nc.scalar.activation(part[s][SUMS][:], memory[s][:, 0, :], ACT.Identity, scale=alpha[:, 0:1])
+            for t in range(SCALAR_WORDS):
+                nc.scalar.activation(part[s][1 + t][:], memory[s][:, t, :], ACT.Identity, scale=alpha[:, t : t + 1])
             return alpha
 
         def attend(s, alpha):
-            for t in range(1, L):
-                k = t % SUMS
-                if t <= SUMS:
-                    nc.vector.tensor_scalar_mul(part[s][k][:], memory[s][:, t, :], alpha[:, t : t + 1])
-                else:
-                    nc.vector.scalar_tensor_tensor(
-                        part[s][k][:],
-                        in0=memory[s][:, t, :],
-                        scalar=alpha[:, t : t + 1],
-                        in1=part[s][k][:],
-                        op0=MULT,
-                        op1=ADD,
-                    )
+            for t in range(SCALAR_WORDS, L):
+                for half in range(HALVES):
+                    cols = slice(half * BANK, (half + 1) * BANK)
+                    if t == SCALAR_WORDS:
+                        nc.vector.tensor_scalar_mul(part[s][0][:, cols], memory[s][:, t, cols], alpha[:, t : t + 1])
+                    else:
+                        nc.vector.scalar_tensor_tensor(
+                            part[s][0][:, cols],
+                            in0=memory[s][:, t, cols],
+                            scalar=alpha[:, t : t + 1],
+                            in1=part[s][0][:, cols],
+                            op0=MULT,
+                            op1=ADD,
+                        )
 
         def add_flipped(s):
-            for k in (SUMS, (L - 2) % SUMS, (L - 1) % SUMS):
+            for k in list(range(1, 1 + SCALAR_WORDS)) + [0]:
                 for half in range(HALVES):
                     for i in range(FLIPS):
                         d = half * FLIPS + i
@@ -180,7 +192,7 @@ def tile_memnet_b_kernel(
                             rhs=identity[:],
                             is_transpose=True,
                             start=False,
-                            stop=(k == (L - 1) % SUMS and i == FLIPS - 1),
+                            stop=(k == 0 and i == FLIPS - 1),
                         )
 
         def round_off(s):
@@ -194,7 +206,7 @@ def tile_memnet_b_kernel(
             return vec
 
         def classify(s, vec):
-            out_ps = psum.tile([P, P], F32, name="out_ps", tag="narrow", bufs=1)
+            out_ps = psum.tile([P, P], F32, name="out_ps", tag=f"narrow{s}", bufs=1)
             for a in range(CB):
                 nc.tensor.matmul(
                     out_ps[:], lhsT=w_out_sb[:, a, :], rhs=vec[:, a, :], start=(a == 0), stop=(a == CB - 1)
@@ -203,25 +215,32 @@ def tile_memnet_b_kernel(
             nc.scalar.activation(out_sb[:], out_ps[:], ACT.Identity, bias=b_out_sb[:, 0:1])
             nc.sync.dma_start(out[:, s * P : (s + 1) * P], out_sb[:])
 
+        first = []
         alphas = []
         for s in range(QB):
+            for j in range(LAST):
+                remember(CB - LAST + j, s, look_up(last_windows[j], s))
             vec = vecs.tile([P, CB, P], BF16, name="vec")
-            nc.scalar.copy(vec[:], aspect_sb[:, :, s * P : (s + 1) * P])
-            alphas.append(weigh(s, vec))
-            for half in range(HALVES):
-                linear(s, vec, half)
-        late = None
+            nc.vector.tensor_copy(vec[:], aspect_sb[:, :, s * P : (s + 1) * P])
+            first.append(vec)
+            alphas.append(weigh(s, project(s, vec)))
+        turned = [
+            [psum.tile([P, FLIPS, P], F32, name=f"turned0{half}", bufs=1) for half in range(HALVES)],
+            [psum.tile([P, FLIPS, P], F32, name=f"turned1{half}", tag="flipped") for half in range(HALVES)],
+        ]
+        for half in range(HALVES):
+            linear(0, first[0], half)
+        waiting = (1, first[1])
         for h in range(HOPS):
             for s in range(QB):
                 attend(s, alphas[s])
                 add_flipped(s)
-                if late is not None:
-                    linear(late[0], late[1], 1)
                 vec = round_off(s)
                 if h < HOPS - 1:
-                    alphas[s] = weigh(s, vec)
-                    linear(s, vec, 0)
-                    late = (s, vec)
+                    alphas[s] = weigh(s, project(s, vec))
                 else:
                     classify(s, vec)
-                    late = None
+                if waiting is not None:
+                    for half in range(HALVES):
+                        linear(waiting[0], waiting[1], half)
+                waiting = (s, vec) if h < HOPS - 1 else None

@@ -16,6 +16,7 @@ FLIPS = BANK // P
 HALVES = C // BANK
 ROWS = 32
 SCALAR_WORDS = 2
+PIECE = 256
 LAST = 2
 
 FLOPS = 2 * C * N + HOPS * (2 * C * Q + 2 * C * C * Q + 2 * C * N) + 2 * C * K * Q
@@ -161,15 +162,21 @@ def tile_memnet_b_kernel(
             nc.vector.reciprocal(inverse[:], total[:])
             alpha = small.tile([P, L], F32, name="alpha")
             nc.scalar.activation(alpha[:], grown[:], ACT.Identity, scale=inverse[:, 0:1])
-            for t in range(SCALAR_WORDS):
-                nc.scalar.activation(part[s][1 + t][:], memory[s][:, t, :], ACT.Identity, scale=alpha[:, t : t + 1])
             return alpha
 
-        def attend(s, alpha):
-            for t in range(SCALAR_WORDS, L):
+        def multiply(s, alpha, scalar_words):
+            for t in range(scalar_words):
+                for piece in range(C // PIECE):
+                    cols = slice(piece * PIECE, (piece + 1) * PIECE)
+                    nc.scalar.activation(
+                        part[s][1 + t][:, cols], memory[s][:, t, cols], ACT.Identity, scale=alpha[:, t : t + 1]
+                    )
+
+        def attend(s, alpha, scalar_words):
+            for t in range(scalar_words, L):
                 for half in range(HALVES):
                     cols = slice(half * BANK, (half + 1) * BANK)
-                    if t == SCALAR_WORDS:
+                    if t == scalar_words:
                         nc.vector.tensor_scalar_mul(part[s][0][:, cols], memory[s][:, t, cols], alpha[:, t : t + 1])
                     else:
                         nc.vector.scalar_tensor_tensor(
@@ -181,8 +188,8 @@ def tile_memnet_b_kernel(
                             op1=ADD,
                         )
 
-        def add_flipped(s):
-            for k in list(range(1, 1 + SCALAR_WORDS)) + [0]:
+        def add_flipped(s, scalar_words):
+            for k in list(range(1, 1 + scalar_words)) + [0]:
                 for half in range(HALVES):
                     for i in range(FLIPS):
                         d = half * FLIPS + i
@@ -233,8 +240,10 @@ def tile_memnet_b_kernel(
         waiting = (1, first[1])
         for h in range(HOPS):
             for s in range(QB):
-                attend(s, alphas[s])
-                add_flipped(s)
+                scalar_words = SCALAR_WORDS if h < HOPS - 1 else SCALAR_WORDS - 1
+                multiply(s, alphas[s], scalar_words)
+                attend(s, alphas[s], scalar_words)
+                add_flipped(s, scalar_words)
                 vec = round_off(s)
                 if h < HOPS - 1:
                     alphas[s] = weigh(s, project(s, vec))

@@ -16,7 +16,7 @@ FLIPS = BANK // P
 HALVES = C // BANK
 ROWS = 32
 SCALAR_WORDS = 2
-PIECE = 256
+PIECE = 512
 LAST = 2
 
 FLOPS = 2 * C * N + HOPS * (2 * C * Q + 2 * C * C * Q + 2 * C * N) + 2 * C * K * Q
@@ -237,19 +237,21 @@ def tile_memnet_b_kernel(
         ]
         for half in range(HALVES):
             linear(0, first[0], half)
-        waiting = (1, first[1])
+        linear(1, first[1], 0)
+        late = (1, first[1])
         for h in range(HOPS):
             for s in range(QB):
                 scalar_words = SCALAR_WORDS if h < HOPS - 1 else SCALAR_WORDS - 1
                 multiply(s, alphas[s], scalar_words)
                 attend(s, alphas[s], scalar_words)
                 add_flipped(s, scalar_words)
+                if late is not None:
+                    linear(late[0], late[1], 1)
                 vec = round_off(s)
                 if h < HOPS - 1:
                     alphas[s] = weigh(s, project(s, vec))
+                    linear(s, vec, 0)
+                    late = (s, vec)
                 else:
                     classify(s, vec)
-                if waiting is not None:
-                    for half in range(HALVES):
-                        linear(waiting[0], waiting[1], half)
-                waiting = (s, vec) if h < HOPS - 1 else None
+                    late = None

@@ -15,8 +15,8 @@ BANK = 512
 FLIPS = BANK // P
 HALVES = C // BANK
 ROWS = 32
-SCALAR_WORDS = 2
-PIECE = 512
+TENSOR_WORDS = (2, 1)
+LAST_HOP_TENSOR_WORDS = ((1, 1), (2, 2))
 LAST = 2
 
 FLOPS = 2 * C * N + HOPS * (2 * C * Q + 2 * C * C * Q + 2 * C * N) + 2 * C * K * Q
@@ -79,7 +79,11 @@ def tile_memnet_b_kernel(
         b_lin_sb, b_out_sb = b_cols[:, 0:CB], b_cols[:, CB : CB + 1]
 
         memory = [held.tile([P, L, C], F32, name=f"memory{s}") for s in range(QB)]
-        part = [[held.tile([P, C], F32, name=f"part{s}{k}") for k in range(1 + SCALAR_WORDS)] for s in range(QB)]
+        part = [
+            [held.tile([P, C], F32, name=f"part{s}{k}") for k in range(1 + max(TENSOR_WORDS + LAST_HOP_TENSOR_WORDS[s]))]
+            for s in range(QB)
+        ]
+        joined = [held.tile([P, C], F32, name=f"joined{s}") for s in range(QB)]
         e_ps = [psum.tile([P, L], F32, name=f"e_ps{s}", bufs=1) for s in range(QB)]
 
         emb_blocks = emb.rearrange("(a p) w -> a p w", p=P)
@@ -158,49 +162,65 @@ def tile_memnet_b_kernel(
             grown = small.tile([P, L], F32, name="grown")
             total = small.tile([P, 1], F32, name="total")
             nc.scalar.activation(grown[:], score[:], ACT.Exp, accum_out=total[:])
+            return grown, total
+
+        def divide(grown, total):
             inverse = small.tile([P, 1], F32, name="inverse")
             nc.vector.reciprocal(inverse[:], total[:])
             alpha = small.tile([P, L], F32, name="alpha")
             nc.scalar.activation(alpha[:], grown[:], ACT.Identity, scale=inverse[:, 0:1])
-            return alpha
+            return inverse, alpha
 
-        def multiply(s, alpha, scalar_words):
-            for t in range(scalar_words):
-                for piece in range(C // PIECE):
-                    cols = slice(piece * PIECE, (piece + 1) * PIECE)
-                    nc.scalar.activation(
-                        part[s][1 + t][:, cols], memory[s][:, t, cols], ACT.Identity, scale=alpha[:, t : t + 1]
-                    )
+        def multiply(s, alpha, tensor_words):
+            for t in range(1 + max(tensor_words)):
+                for half in range(HALVES):
+                    if t <= tensor_words[half]:
+                        cols = slice(half * BANK, (half + 1) * BANK)
+                        product = joined[s] if t == 0 else part[s][t]
+                        nc.scalar.activation(
+                            product[:, cols], memory[s][:, t, cols], ACT.Identity, scale=alpha[:, t : t + 1]
+                        )
 
-        def attend(s, alpha, scalar_words):
-            for t in range(scalar_words, L):
+        def attend(s, grown, inverse, tensor_words):
+            for t in range(1 + min(tensor_words), L):
                 for half in range(HALVES):
                     cols = slice(half * BANK, (half + 1) * BANK)
-                    if t == scalar_words:
-                        nc.vector.tensor_scalar_mul(part[s][0][:, cols], memory[s][:, t, cols], alpha[:, t : t + 1])
-                    else:
+                    if t == 1 + tensor_words[half]:
+                        nc.vector.tensor_scalar_mul(part[s][0][:, cols], memory[s][:, t, cols], grown[:, t : t + 1])
+                    elif t > 1 + tensor_words[half]:
                         nc.vector.scalar_tensor_tensor(
                             part[s][0][:, cols],
                             in0=memory[s][:, t, cols],
-                            scalar=alpha[:, t : t + 1],
+                            scalar=grown[:, t : t + 1],
                             in1=part[s][0][:, cols],
                             op0=MULT,
                             op1=ADD,
                         )
+            for half in range(HALVES):
+                cols = slice(half * BANK, (half + 1) * BANK)
+                nc.vector.scalar_tensor_tensor(
+                    part[s][0][:, cols],
+                    in0=part[s][0][:, cols],
+                    scalar=inverse[:, 0:1],
+                    in1=joined[s][:, cols],
+                    op0=MULT,
+                    op1=ADD,
+                )
 
-        def add_flipped(s, scalar_words):
-            for k in list(range(1, 1 + scalar_words)) + [0]:
+        def add_flipped(s, tensor_words):
+            for k in list(range(1, 1 + max(tensor_words))) + [0]:
                 for half in range(HALVES):
-                    for i in range(FLIPS):
-                        d = half * FLIPS + i
-                        nc.tensor.matmul(
-                            turned[s][half][:, i, :],
-                            lhsT=part[s][k][:, d * P : (d + 1) * P],
-                            rhs=identity[:],
-                            is_transpose=True,
-                            start=False,
-                            stop=(k == 0 and i == FLIPS - 1),
-                        )
+                    if k <= tensor_words[half]:
+                        for i in range(FLIPS):
+                            d = half * FLIPS + i
+                            nc.tensor.matmul(
+                                turned[s][half][:, i, :],
+                                lhsT=part[s][k][:, d * P : (d + 1) * P],
+                                rhs=identity[:],
+                                is_transpose=True,
+                                start=False,
+                                stop=(k == 0 and i == FLIPS - 1),
+                            )
 
         def round_off(s):
             vec = vecs.tile([P, CB, P], BF16, name="vec")
@@ -223,14 +243,14 @@ def tile_memnet_b_kernel(
             nc.sync.dma_start(out[:, s * P : (s + 1) * P], out_sb[:])
 
         first = []
-        alphas = []
+        weights = []
         for s in range(QB):
             for j in range(LAST):
                 remember(CB - LAST + j, s, look_up(last_windows[j], s))
             vec = vecs.tile([P, CB, P], BF16, name="vec")
             nc.vector.tensor_copy(vec[:], aspect_sb[:, :, s * P : (s + 1) * P])
             first.append(vec)
-            alphas.append(weigh(s, project(s, vec)))
+            weights.append(weigh(s, project(s, vec)))
         turned = [
             [psum.tile([P, FLIPS, P], F32, name=f"turned0{half}", bufs=1) for half in range(HALVES)],
             [psum.tile([P, FLIPS, P], F32, name=f"turned1{half}", tag="flipped") for half in range(HALVES)],
@@ -241,15 +261,17 @@ def tile_memnet_b_kernel(
         late = (1, first[1])
         for h in range(HOPS):
             for s in range(QB):
-                scalar_words = SCALAR_WORDS if h < HOPS - 1 else SCALAR_WORDS - 1
-                multiply(s, alphas[s], scalar_words)
-                attend(s, alphas[s], scalar_words)
-                add_flipped(s, scalar_words)
+                tensor_words = TENSOR_WORDS if h < HOPS - 1 else LAST_HOP_TENSOR_WORDS[s]
+                grown, total = weights[s]
+                inverse, alpha = divide(grown, total)
+                multiply(s, alpha, tensor_words)
+                attend(s, grown, inverse, tensor_words)
+                add_flipped(s, tensor_words)
                 if late is not None:
                     linear(late[0], late[1], 1)
                 vec = round_off(s)
                 if h < HOPS - 1:
-                    alphas[s] = weigh(s, project(s, vec))
+                    weights[s] = weigh(s, project(s, vec))
                     linear(s, vec, 0)
                     late = (s, vec)
                 else:

@@ -15,7 +15,8 @@ BANK = 512
 FLIPS = BANK // P
 HALVES = C // BANK
 ROWS = 32
-TENSOR_WORDS = (2, 1)
+TENSOR_WORDS = ((2, 2), (2, 1))
+FIRST_HOP_TENSOR_WORDS = ((1, 1), (2, 1))
 LAST_HOP_TENSOR_WORDS = ((1, 1), (2, 2))
 LAST = 2
 
@@ -80,7 +81,7 @@ def tile_memnet_b_kernel(
 
         memory = [held.tile([P, L, C], F32, name=f"memory{s}") for s in range(QB)]
         part = [
-            [held.tile([P, C], F32, name=f"part{s}{k}") for k in range(1 + max(TENSOR_WORDS + LAST_HOP_TENSOR_WORDS[s]))]
+            [held.tile([P, C], F32, name=f"part{s}{k}") for k in range(1 + max(TENSOR_WORDS[s] + LAST_HOP_TENSOR_WORDS[s]))]
             for s in range(QB)
         ]
         joined = [held.tile([P, C], F32, name=f"joined{s}") for s in range(QB)]
@@ -261,7 +262,7 @@ def tile_memnet_b_kernel(
         late = (1, first[1])
         for h in range(HOPS):
             for s in range(QB):
-                tensor_words = TENSOR_WORDS if h < HOPS - 1 else LAST_HOP_TENSOR_WORDS[s]
+                tensor_words = (FIRST_HOP_TENSOR_WORDS if h == 0 else LAST_HOP_TENSOR_WORDS if h == HOPS - 1 else TENSOR_WORDS)[s]
                 grown, total = weights[s]
                 inverse, alpha = divide(grown, total)
                 multiply(s, alpha, tensor_words)

@@ -15,9 +15,9 @@ BANK = 512
 FLIPS = BANK // P
 HALVES = C // BANK
 ROWS = 32
-TENSOR_WORDS = ((2, 2), (2, 1))
-FIRST_HOP_TENSOR_WORDS = ((1, 1), (2, 1))
-LAST_HOP_TENSOR_WORDS = ((1, 1), (2, 2))
+SHARED = 768
+FIRST_HOP_SHARED = (0, SHARED)
+LAST_HOP_SHARED = (0, C)
 LAST = 2
 
 FLOPS = 2 * C * N + HOPS * (2 * C * Q + 2 * C * C * Q + 2 * C * N) + 2 * C * K * Q
@@ -80,10 +80,7 @@ def tile_memnet_b_kernel(
         b_lin_sb, b_out_sb = b_cols[:, 0:CB], b_cols[:, CB : CB + 1]
 
         memory = [held.tile([P, L, C], F32, name=f"memory{s}") for s in range(QB)]
-        part = [
-            [held.tile([P, C], F32, name=f"part{s}{k}") for k in range(1 + max(TENSOR_WORDS[s] + LAST_HOP_TENSOR_WORDS[s]))]
-            for s in range(QB)
-        ]
+        part = [[held.tile([P, C], F32, name=f"part{s}{k}") for k in range(3)] for s in range(QB)]
         joined = [held.tile([P, C], F32, name=f"joined{s}") for s in range(QB)]
         e_ps = [psum.tile([P, L], F32, name=f"e_ps{s}", bufs=1) for s in range(QB)]
 
@@ -172,23 +169,25 @@ def tile_memnet_b_kernel(
             nc.scalar.activation(alpha[:], grown[:], ACT.Identity, scale=inverse[:, 0:1])
             return inverse, alpha
 
-        def multiply(s, alpha, tensor_words):
-            for t in range(1 + max(tensor_words)):
-                for half in range(HALVES):
-                    if t <= tensor_words[half]:
-                        cols = slice(half * BANK, (half + 1) * BANK)
-                        product = joined[s] if t == 0 else part[s][t]
+        def ranges(shared):
+            cut = shared if 0 < shared < C else BANK
+            return [(slice(0, cut), cut <= shared), (slice(cut, C), C <= shared)]
+
+        def multiply(s, alpha, shared):
+            for t, product in enumerate([joined[s], part[s][1], part[s][2]]):
+                for cols, scalar_has_word_2 in ranges(shared):
+                    if t < 2 or scalar_has_word_2:
                         nc.scalar.activation(
                             product[:, cols], memory[s][:, t, cols], ACT.Identity, scale=alpha[:, t : t + 1]
                         )
 
-        def attend(s, grown, inverse, tensor_words):
-            for t in range(1 + min(tensor_words), L):
-                for half in range(HALVES):
-                    cols = slice(half * BANK, (half + 1) * BANK)
-                    if t == 1 + tensor_words[half]:
+        def attend(s, grown, inverse, shared):
+            for t in range(2, L):
+                for cols, scalar_has_word_2 in ranges(shared):
+                    first = 3 if scalar_has_word_2 else 2
+                    if t == first:
                         nc.vector.tensor_scalar_mul(part[s][0][:, cols], memory[s][:, t, cols], grown[:, t : t + 1])
-                    elif t > 1 + tensor_words[half]:
+                    elif t > first:
                         nc.vector.scalar_tensor_tensor(
                             part[s][0][:, cols],
                             in0=memory[s][:, t, cols],
@@ -197,8 +196,7 @@ def tile_memnet_b_kernel(
                             op0=MULT,
                             op1=ADD,
                         )
-            for half in range(HALVES):
-                cols = slice(half * BANK, (half + 1) * BANK)
+            for cols, scalar_has_word_2 in ranges(shared):
                 nc.vector.scalar_tensor_tensor(
                     part[s][0][:, cols],
                     in0=part[s][0][:, cols],
@@ -208,20 +206,17 @@ def tile_memnet_b_kernel(
                     op1=ADD,
                 )
 
-        def add_flipped(s, tensor_words):
-            for k in list(range(1, 1 + max(tensor_words))) + [0]:
-                for half in range(HALVES):
-                    if k <= tensor_words[half]:
-                        for i in range(FLIPS):
-                            d = half * FLIPS + i
-                            nc.tensor.matmul(
-                                turned[s][half][:, i, :],
-                                lhsT=part[s][k][:, d * P : (d + 1) * P],
-                                rhs=identity[:],
-                                is_transpose=True,
-                                start=False,
-                                stop=(k == 0 and i == FLIPS - 1),
-                            )
+        def add_flipped(s, shared):
+            for k, features in ((1, C), (2, shared), (0, C)):
+                for d in range(features // P):
+                    nc.tensor.matmul(
+                        turned[s][d // FLIPS][:, d % FLIPS, :],
+                        lhsT=part[s][k][:, d * P : (d + 1) * P],
+                        rhs=identity[:],
+                        is_transpose=True,
+                        start=False,
+                        stop=(k == 0 and d % FLIPS == FLIPS - 1),
+                    )
 
         def round_off(s):
             vec = vecs.tile([P, CB, P], BF16, name="vec")
@@ -262,12 +257,12 @@ def tile_memnet_b_kernel(
         late = (1, first[1])
         for h in range(HOPS):
             for s in range(QB):
-                tensor_words = (FIRST_HOP_TENSOR_WORDS if h == 0 else LAST_HOP_TENSOR_WORDS if h == HOPS - 1 else TENSOR_WORDS)[s]
+                shared = FIRST_HOP_SHARED[s] if h == 0 else LAST_HOP_SHARED[s] if h == HOPS - 1 else SHARED
                 grown, total = weights[s]
                 inverse, alpha = divide(grown, total)
-                multiply(s, alpha, tensor_words)
-                attend(s, grown, inverse, tensor_words)
-                add_flipped(s, tensor_words)
+                multiply(s, alpha, shared)
+                attend(s, grown, inverse, shared)
+                add_flipped(s, shared)
                 if late is not None:
                     linear(late[0], late[1], 1)
                 vec = round_off(s)

import concourse.mybir as mybir
from concourse.masks import make_identity

F32, BF16, U16 = mybir.dt.float32, mybir.dt.bfloat16, mybir.dt.uint16
MULT, ADD = mybir.AluOpType.mult, mybir.AluOpType.add
ACT = mybir.ActivationFunctionType

P = 128
C, W, N, Q, L, K, HOPS = 1024, 4096, 2048, 256, 8, 128, 6
B_ATT = 0.5
CB = C // P
QB = Q // P
NB = N // QB
BANK = 512
FLIPS = BANK // P
HALVES = C // BANK
ROWS = 32
SHARED = 768
FIRST_HOP_SHARED = (0, SHARED)
LAST_HOP_SHARED = (0, C)
LAST = 2

FLOPS = 2 * C * N + HOPS * (2 * C * Q + 2 * C * C * Q + 2 * C * N) + 2 * C * K * Q


def tile_memnet_b_kernel(
    tc, emb, v_loc, aspect, w_mem, w_vec, w_lin, b_lin, w_out, b_out, offs, out
):
    nc = tc.nc
    with (
        tc.tile_pool(name="held", bufs=1) as held,
        tc.tile_pool(name="windows", bufs=3) as windows,
        tc.tile_pool(name="picked", bufs=4) as picked,
        tc.tile_pool(name="vecs", bufs=2 * QB) as vecs,
        tc.tile_pool(name="small", bufs=2 * QB) as small,
        tc.tile_pool(name="results", bufs=QB) as results,
        tc.psum_pool(name="psum", bufs=2) as psum,
    ):
        offsets = held.tile([P, N // 16], U16, name="offsets")
        nc.sync.dma_start(offsets[:], offs)
        identity = held.tile([P, P], F32, name="identity")
        make_identity(nc, identity[:])

        vloc_rows = held.tile([ROWS, P], F32, name="vloc_rows")
        for copy in range(ROWS * P // N):
            nc.sync.dma_start(
                vloc_rows[copy * N // P : (copy + 1) * N // P, :], v_loc.rearrange("o (r p) -> (o r) p", p=P)
            )
        vloc_ps = psum.tile([P, N // P], F32, name="vloc_ps", tag="narrow0", bufs=1)
        nc.tensor.matmul(vloc_ps[:], lhsT=vloc_rows[:], rhs=identity[0:ROWS, 0 : N // P], start=True, stop=True)
        vloc_cols = held.tile([P, N // P], F32, name="vloc_cols")
        nc.vector.tensor_copy(vloc_cols[:], vloc_ps[:])
        vloc_bc = held.tile([P, N], F32, name="vloc_bc")
        for b in range(N // BANK):
            spread = psum.tile([P, FLIPS, P], F32, name="spread", tag="flipped")
            for i in range(FLIPS):
                r = b * FLIPS + i
                nc.tensor.transpose(spread[:, i, :], vloc_cols[:, r : r + 1].to_broadcast([P, P]), identity[:])
            nc.scalar.copy(vloc_bc[:, b * BANK : (b + 1) * BANK], spread[:])

        w_rows = held.tile([ROWS, P], BF16, name="w_rows")
        nc.vector.memset(w_rows[:], 0.0)
        nc.sync.dma_start(w_rows[0:CB, :], w_mem.rearrange("(a p) o -> a (p o)", p=P))
        nc.sync.dma_start(w_rows[CB : 2 * CB, :], w_vec.rearrange("(a p) o -> a (p o)", p=P))
        b_rows = held.tile([ROWS, P], F32, name="b_rows")
        nc.vector.memset(b_rows[:], 0.0)
        nc.sync.dma_start(b_rows[0:CB, :], b_lin.rearrange("(a p) o -> a (p o)", p=P))
        nc.sync.dma_start(b_rows[CB : CB + 1, :], b_out.rearrange("k o -> o k"))
        identity_bf = held.tile([ROWS, 2 * CB], BF16, name="identity_bf")
        nc.vector.tensor_copy(identity_bf[:], identity[0:ROWS, 0 : 2 * CB])
        w_ps = psum.tile([P, 2 * CB], F32, name="w_ps", tag="narrow0", bufs=1)
        nc.tensor.matmul(w_ps[:], lhsT=w_rows[:], rhs=identity_bf[:], start=True, stop=True)
        w_cols = held.tile([P, 2 * CB], BF16, name="w_cols")
        nc.vector.tensor_copy(w_cols[:], w_ps[:])
        b_ps = psum.tile([P, CB + 1], F32, name="b_ps", tag="narrow1", bufs=1)
        nc.tensor.matmul(b_ps[:], lhsT=b_rows[:], rhs=identity[0:ROWS, 0 : CB + 1], start=True, stop=True)
        b_cols = held.tile([P, CB + 1], F32, name="b_cols")
        nc.vector.tensor_copy(b_cols[:], b_ps[:])
        w_mem_sb, w_vec_sb = w_cols[:, 0:CB], w_cols[:, CB : 2 * CB]
        b_lin_sb, b_out_sb = b_cols[:, 0:CB], b_cols[:, CB : CB + 1]

        memory = [held.tile([P, L, C], F32, name=f"memory{s}") for s in range(QB)]
        part = [[held.tile([P, C], F32, name=f"part{s}{k}") for k in range(3)] for s in range(QB)]
        joined = [held.tile([P, C], F32, name=f"joined{s}") for s in range(QB)]
        e_ps = [psum.tile([P, L], F32, name=f"e_ps{s}", bufs=1) for s in range(QB)]

        emb_blocks = emb.rearrange("(a p) w -> a p w", p=P)

        def load(a):
            window = windows.tile([P, W], F32, name="window")
            nc.sync.dma_start(window[:], emb_blocks[a])
            return window

        def look_up(window, s):
            ext = picked.tile([P, NB], F32, name="ext")
            nc.vector.tensor_tensor(
                ext[:],
                window[:].indirect(offsets[:, s * NB // 16 : (s + 1) * NB // 16]),
                vloc_bc[:, s * NB : (s + 1) * NB],
                MULT,
            )
            return ext

        def remember(a, s, ext):
            ext_bf = picked.tile([P, NB], BF16, name="ext_bf")
            nc.scalar.copy(ext_bf[:], ext[:])
            for g in range(L // FLIPS):
                flipped = psum.tile([P, FLIPS, P], F32, name="flipped")
                for i in range(FLIPS):
                    nc.tensor.transpose(flipped[:, i, :], ext[:, g * FLIPS + i : NB : L], identity[:])
                nc.scalar.copy(memory[s][:, g * FLIPS : (g + 1) * FLIPS, a * P : (a + 1) * P], flipped[:])
            for t in range(L):
                nc.tensor.matmul(
                    e_ps[s][:, t : t + 1],
                    lhsT=ext_bf[:, t:NB:L],
                    rhs=w_mem_sb[:, a : a + 1],
                    start=(a == 0 and t == 0),
                    stop=(a == CB - 1 and t == L - 1),
                )

        for a in range(CB - LAST):
            window = load(a)
            for s in range(QB):
                remember(a, s, look_up(window, s))
        last_windows = [load(a) for a in range(CB - LAST, CB)]

        aspect_sb = held.tile([P, CB, Q], F32, name="aspect_sb")
        nc.sync.dma_start(aspect_sb[:], aspect.rearrange("(a p) q -> p a q", p=P))
        w_lin_sb = [held.tile([P, CB, BANK], BF16, name=f"w_lin_sb{half}") for half in range(HALVES)]
        w_lin_halves = w_lin.rearrange("(a p) (half d) -> half p a d", p=P, half=HALVES)
        for half in range(HALVES):
            nc.sync.dma_start(w_lin_sb[half][:], w_lin_halves[half])
        w_out_sb = held.tile([P, CB, K], BF16, name="w_out_sb")
        nc.sync.dma_start(w_out_sb[:], w_out.rearrange("(a p) k -> p a k", p=P))

        def linear(s, vec, half):
            for i in range(FLIPS):
                for a in range(CB):
                    nc.tensor.matmul(
                        turned[s][half][:, i, :],
                        lhsT=w_lin_sb[half][:, a, i * P : (i + 1) * P],
                        rhs=vec[:, a, :],
                        start=(i == 0 and a == 0),
                        stop=False,
                    )

        def project(s, vec):
            u_ps = psum.tile([P, 1], F32, name="u_ps", tag=f"narrow{s}", bufs=1)
            for a in range(CB):
                nc.tensor.matmul(
                    u_ps[:], lhsT=vec[:, a, :], rhs=w_vec_sb[:, a : a + 1], start=(a == 0), stop=(a == CB - 1)
                )
            u_sb = small.tile([P, 1], F32, name="u_sb")
            nc.scalar.activation(u_sb[:], u_ps[:], ACT.Identity, bias=B_ATT)
            return u_sb

        def weigh(s, u_sb):
            score = small.tile([P, L], F32, name="score")
            nc.scalar.activation(score[:], e_ps[s][:], ACT.Tanh, bias=u_sb[:, 0:1])
            grown = small.tile([P, L], F32, name="grown")
            total = small.tile([P, 1], F32, name="total")
            nc.scalar.activation(grown[:], score[:], ACT.Exp, accum_out=total[:])
            return grown, total

        def divide(grown, total):
            inverse = small.tile([P, 1], F32, name="inverse")
            nc.vector.reciprocal(inverse[:], total[:])
            alpha = small.tile([P, L], F32, name="alpha")
            nc.scalar.activation(alpha[:], grown[:], ACT.Identity, scale=inverse[:, 0:1])
            return inverse, alpha

        def ranges(shared):
            cut = shared if 0 < shared < C else BANK
            return [(slice(0, cut), cut <= shared), (slice(cut, C), C <= shared)]

        def multiply(s, alpha, shared):
            for t, product in enumerate([joined[s], part[s][1], part[s][2]]):
                for cols, scalar_has_word_2 in ranges(shared):
                    if t < 2 or scalar_has_word_2:
                        nc.scalar.activation(
                            product[:, cols], memory[s][:, t, cols], ACT.Identity, scale=alpha[:, t : t + 1]
                        )

        def attend(s, grown, inverse, shared):
            for t in range(2, L):
                for cols, scalar_has_word_2 in ranges(shared):
                    first = 3 if scalar_has_word_2 else 2
                    if t == first:
                        nc.vector.tensor_scalar_mul(part[s][0][:, cols], memory[s][:, t, cols], grown[:, t : t + 1])
                    elif t > first:
                        nc.vector.scalar_tensor_tensor(
                            part[s][0][:, cols],
                            in0=memory[s][:, t, cols],
                            scalar=grown[:, t : t + 1],
                            in1=part[s][0][:, cols],
                            op0=MULT,
                            op1=ADD,
                        )
            for cols, scalar_has_word_2 in ranges(shared):
                nc.vector.scalar_tensor_tensor(
                    part[s][0][:, cols],
                    in0=part[s][0][:, cols],
                    scalar=inverse[:, 0:1],
                    in1=joined[s][:, cols],
                    op0=MULT,
                    op1=ADD,
                )

        def add_flipped(s, shared):
            for k, features in ((1, C), (2, shared), (0, C)):
                for d in range(features // P):
                    nc.tensor.matmul(
                        turned[s][d // FLIPS][:, d % FLIPS, :],
                        lhsT=part[s][k][:, d * P : (d + 1) * P],
                        rhs=identity[:],
                        is_transpose=True,
                        start=False,
                        stop=(k == 0 and d % FLIPS == FLIPS - 1),
                    )

        def round_off(s):
            vec = vecs.tile([P, CB, P], BF16, name="vec")
            for half in range(HALVES):
                for i in range(FLIPS):
                    d = half * FLIPS + i
                    nc.scalar.activation(
                        vec[:, d, :], turned[s][half][:, i, :], ACT.Identity, bias=b_lin_sb[:, d : d + 1]
                    )
            return vec

        def classify(s, vec):
            out_ps = psum.tile([P, P], F32, name="out_ps", tag=f"narrow{s}", bufs=1)
            for a in range(CB):
                nc.tensor.matmul(
                    out_ps[:], lhsT=w_out_sb[:, a, :], rhs=vec[:, a, :], start=(a == 0), stop=(a == CB - 1)
                )
            out_sb = results.tile([P, P], F32, name="out_sb")
            nc.scalar.activation(out_sb[:], out_ps[:], ACT.Identity, bias=b_out_sb[:, 0:1])
            nc.sync.dma_start(out[:, s * P : (s + 1) * P], out_sb[:])

        first = []
        weights = []
        for s in range(QB):
            for j in range(LAST):
                remember(CB - LAST + j, s, look_up(last_windows[j], s))
            vec = vecs.tile([P, CB, P], BF16, name="vec")
            nc.vector.tensor_copy(vec[:], aspect_sb[:, :, s * P : (s + 1) * P])
            first.append(vec)
            weights.append(weigh(s, project(s, vec)))
        turned = [
            [psum.tile([P, FLIPS, P], F32, name=f"turned0{half}", bufs=1) for half in range(HALVES)],
            [psum.tile([P, FLIPS, P], F32, name=f"turned1{half}", tag="flipped") for half in range(HALVES)],
        ]
        for half in range(HALVES):
            linear(0, first[0], half)
        linear(1, first[1], 0)
        late = (1, first[1])
        for h in range(HOPS):
            for s in range(QB):
                shared = FIRST_HOP_SHARED[s] if h == 0 else LAST_HOP_SHARED[s] if h == HOPS - 1 else SHARED
                grown, total = weights[s]
                inverse, alpha = divide(grown, total)
                multiply(s, alpha, shared)
                attend(s, grown, inverse, shared)
                add_flipped(s, shared)
                if late is not None:
                    linear(late[0], late[1], 1)
                vec = round_off(s)
                if h < HOPS - 1:
                    weights[s] = weigh(s, project(s, vec))
                    linear(s, vec, 0)
                    late = (s, vec)
                else:
                    classify(s, vec)
                    late = None
